import numpy as np
import ml_dtypes


def mxq(x, axis, fmt="e4m3"):
    dtype, down = {"e4m3": (ml_dtypes.float8_e4m3fn, 7), "e5m2": (ml_dtypes.float8_e5m2, 14)}[fmt]
    v = np.moveaxis(np.asarray(x, np.float32).astype(ml_dtypes.bfloat16).astype(np.float64), axis, -1)
    blocks = v.reshape(v.shape[:-1] + (-1, 32))
    amax = np.abs(blocks).max(-1, keepdims=True)
    byte = np.maximum(np.where(amax > 0, np.frexp(amax)[1] - 1 + 127, 0) - down, 1)
    scale = np.exp2(byte - 127.0)
    codes = (blocks / scale).astype(np.float32).astype(dtype).astype(np.float64)
    return np.moveaxis((codes * scale).reshape(v.shape), -1, axis)


WIDE = False


def mx_kscale(k):
    if not WIDE:
        return np.ones(k)
    levels = np.array([10, -10, 5, -5, 0])
    a = np.random.permutation(np.resize(levels, k // 512 * 4)).reshape(k // 512, 4)
    idx = np.arange(k)
    return np.exp2(a[idx // 512, idx % 128 // 32])


BF16 = ml_dtypes.bfloat16


def bf(x):
    return np.asarray(x, np.float32).astype(BF16)


def f64(x):
    return np.asarray(x).astype(np.float64)


E2M1 = np.array([0.0, 0.5, 1.0, 1.5, 2.0, 3.0, 4.0, 6.0, -0.0, -0.5, -1.0, -1.5, -2.0, -3.0, -4.0, -6.0])


def pack_weight(w, fmt):
    k, n = w.shape
    w = f64(bf(w)).reshape(k // 32, 32, n)
    amax = np.abs(w).max(1)
    if fmt == "e4m3":
        byte = np.frexp(amax)[1] - 1 + 127 - 7
    else:
        mant, ex = np.frexp(amax / 6.0)
        byte = np.where(mant > 0.5, ex, ex - 1) + 127
    byte = np.clip(np.where(amax > 0, byte, 1), 1, 254)
    scaled = (w * np.exp2(127.0 - byte)[:, None, :]).reshape(k, n).astype(np.float32)
    by_word = np.ascontiguousarray(scaled.reshape(k // 512, 128, 4, n).transpose(0, 1, 3, 2))
    if fmt == "e4m3":
        words = by_word.astype(ml_dtypes.float8_e4m3fn).view(np.uint8)
    else:
        c = by_word.astype(ml_dtypes.float4_e2m1fn).view(np.uint8) & 0xF
        words = c[..., 0::2] | (c[..., 1::2] << 4)
    return np.ascontiguousarray(words), np.ascontiguousarray(byte.astype(np.uint8).reshape(k // 512, 16, n))


def unpack_weight(words, scales, fmt):
    g, p, n, _ = words.shape
    if fmt == "e4m3":
        vals = np.ascontiguousarray(words).view(ml_dtypes.float8_e4m3fn).astype(np.float64)
    else:
        nib = np.empty((g, p, n, 4), np.uint8)
        nib[..., 0::2] = words & 0xF
        nib[..., 1::2] = words >> 4
        vals = E2M1[nib]
    vals = vals * np.repeat(np.exp2(scales.astype(np.float64) - 127.0), 8, axis=1)[..., None]
    return vals.transpose(0, 1, 3, 2).reshape(g * 512, n)


N, M, C, S, D = 1024, 1536, 64, 7, 1024


def setup_inputs():
    s = mx_kscale(D)
    hid = bf(np.maximum(np.random.standard_normal((N, D)), 0.0) * s)
    ref_hid = bf(np.maximum(np.random.standard_normal((M, D)), 0.0) * s)
    W1_words, W1_scales = pack_weight(np.random.standard_normal((D, D)) * 0.2 / np.sqrt(D) / s[:, None], "e4m3")
    b1 = bf(np.random.standard_normal(D) * 0.05)
    return {"hid": hid,
            "ref_hid": ref_hid,
            "W1_words": W1_words,
            "W1_scales": W1_scales,
            "b1": b1}


def reference(hid, ref_hid, W1_words, W1_scales, b1):
    wq = unpack_weight(W1_words, W1_scales, "e4m3")
    h = (mxq(f64(hid), 1, "e4m3") @ wq) + f64(b1)
    rh = (mxq(f64(ref_hid), 1, "e4m3") @ wq) + f64(b1)
    prod = mxq(h, 1, "e4m3") @ mxq(rh, 1, "e4m3").T
    zcol = np.zeros((prod.shape[0], 1))
    return np.concatenate([zcol, prod], axis=1)

@@ -1,0 +1,194 @@
+from contextlib import ExitStack
+
+import concourse.mybir as mybir
+from concourse.masks import make_identity
+
+F32 = mybir.dt.float32
+BF16 = mybir.dt.bfloat16
+I32 = mybir.dt.int32
+U32 = mybir.dt.uint32
+U8 = mybir.dt.uint8
+FP8X4 = mybir.dt.float8_e4m3fn_x4
+IDENTITY = mybir.ActivationFunctionType.Identity
+
+P = 128
+PACK = 4
+K_PASS = P * PACK
+D = 1024
+PASSES = D // K_PASS
+N_HID = 1024
+N_REF = 1536
+CHUNK = 512
+TILES = CHUNK // P
+HALF = CHUNK // 2
+REF_CHUNKS = N_REF // CHUNK
+HID_CHUNKS = N_HID // CHUNK
+HID_TILES = N_HID // P
+OUT_COLS = 1 + N_REF
+OUT_PITCH = 1544
+
+FLOPS = 2 * (N_HID + N_REF) * D * D + 2 * N_HID * N_REF * D
+
+
+def transpose_and_quantise(nc, psum, stage, identity, x_rows, x_codes, x_scales):
+    for g in range(PASSES):
+        grouped = stage.tile([P, CHUNK, PACK], BF16, tag="grouped_x", align_bytes=64)
+        for half in range(CHUNK // HALF):
+            bank = psum.tile([P, 2, HALF], F32, tag="bank")
+            for u in range(2):
+                for i in range(HALF // P):
+                    words = x_rows[:, half * (HALF // P) + i, :].bitcast(F32)
+                    nc.tensor.transpose(
+                        bank[:, u, i * P : (i + 1) * P],
+                        words[:, 256 * g + u : 256 * (g + 1) : 2],
+                        identity[:],
+                    )
+            rows = grouped[:, half * HALF : (half + 1) * HALF, :]
+            pairs = rows.rearrange("p r t -> p (r t)").bitcast(F32).rearrange("p (r u) -> p r u", u=2)
+            if half == 0:
+                nc.vector.tensor_copy(out=pairs, in_=bank[:].rearrange("p u r -> p r u"))
+            else:
+                nc.scalar.copy(out=pairs, in_=bank[:].rearrange("p u r -> p r u"))
+        nc.vector.quantize_mx(
+            out=x_codes[:, g, :].bitcast(FP8X4),
+            scales=x_scales[:, g, :],
+            in_=grouped[:].rearrange("p r t -> p (r t)"),
+        )
+
+
+def project(nc, psum, stage, w_codes, w_scales, bias, x_codes, x_scales, G):
+    planes = stage.tile([P, PACK, CHUNK], BF16, tag="planes")
+    for t in range(PACK):
+        m = PACK * G + t
+        features = slice(m * P, (m + 1) * P)
+        acc = psum.tile([P, CHUNK], F32, tag="bank")
+        for g in range(PASSES):
+            nc.tensor.matmul_mx(
+                out=acc[:],
+                lhsT=w_codes[:, g, features].bitcast(FP8X4),
+                lhsT_scale=w_scales[:, g, features],
+                rhs=x_codes[:, g, :].bitcast(FP8X4),
+                rhs_scale=x_scales[:, g, :],
+                start=(g == 0),
+                stop=(g == PASSES - 1),
+            )
+        nc.scalar.activation(out=planes[:, t, :], in_=acc[:], func=IDENTITY, bias=bias[:, m : m + 1])
+    return planes
+
+
+def regroup_and_quantise(nc, stage, planes, codes, scales):
+    grouped = stage.tile([P, CHUNK, PACK], BF16, tag="grouped_h", align_bytes=64)
+    nc.vector.tensor_copy(
+        out=grouped[:].rearrange("p (c i) t -> p c t i", i=4),
+        in_=planes[:].rearrange("p t (c i) -> p c t i", i=4),
+    )
+    nc.vector.quantize_mx(
+        out=codes.bitcast(FP8X4),
+        scales=scales,
+        in_=grouped[:].rearrange("p r t -> p (r t)"),
+    )
+
+
+def tile_trackhead_pa_kernel(tc, hid, ref_hid, W1_words, W1_scales, b1, out):
+    nc = tc.nc
+    with ExitStack() as ctx:
+        keep = ctx.enter_context(tc.tile_pool(name="keep", bufs=1))
+        stage = ctx.enter_context(tc.tile_pool(name="stage", bufs=3))
+        psum = ctx.enter_context(tc.psum_pool(name="psum", bufs=8))
+        ctx.enter_context(tc.manual_schedule())
+
+        ref_sb = keep.tile([P, N_REF // P, D], BF16)
+        hid_sb = keep.tile([P, HID_TILES, D], BF16)
+        w_codes = keep.tile([P, PASSES, D], U32, align_bytes=64)
+        w_scales = keep.tile([P, PASSES, D], U8, align_bytes=64)
+        rh_codes = keep.tile([P, PASSES, N_REF], U32, align_bytes=64)
+        rh_scales = keep.tile([P, PASSES, N_REF], U8, align_bytes=64)
+        h_codes = keep.tile([P, PASSES, N_HID], U32, align_bytes=64)
+        h_scales = keep.tile([P, PASSES, N_HID], U8, align_bytes=64)
+        out_sb = keep.tile([P, HID_TILES, OUT_PITCH], F32)
+        identity = keep.tile([P, P], F32)
+        bias_rows = keep.tile([P, P], BF16)
+        bias_rows_f32 = keep.tile([P, P], F32)
+        bias = keep.tile([P, D // P], F32)
+
+        nc.vector.memset(w_scales[:].rearrange("p g n -> p (g n)").bitcast(I32), 0)
+        nc.vector.memset(bias_rows[:], 0.0)
+        make_identity(nc, identity[:])
+        nc.gpsimd.memset(out_sb[:, :, 0:8], 0.0)
+
+        ref_view = ref_hid.rearrange("(i p) k -> p i k", p=P)
+        hid_view = hid.rearrange("(p j) k -> p j k", j=HID_TILES)
+        out_view = out.rearrange("(p j) n -> p j n", j=HID_TILES)
+
+        for i in range(TILES):
+            nc.sync.dma_start(out=ref_sb[:, i, :], in_=ref_view[:, i, :])
+        nc.sync.dma_start(out=bias_rows[0 : D // P, :], in_=b1.rearrange("(m p) -> m p", p=P))
+        for Q in range(4):
+            nc.sync.dma_start(
+                out=w_scales[32 * Q : 32 * Q + 4, :, :].bitcast(I32),
+                in_=W1_scales[:, 4 * Q : 4 * Q + 4, :].rearrange("g r n -> r g n").bitcast(I32),
+            )
+        for g in range(PASSES):
+            nc.sync.dma_start(
+                out=w_codes[:, g, :].bitcast(I32),
+                in_=W1_words[g].rearrange("p n t -> p (n t)").bitcast(I32),
+            )
+        for i in range(TILES, N_REF // P):
+            nc.sync.dma_start(out=ref_sb[:, i, :], in_=ref_view[:, i, :])
+        for c in range(HID_CHUNKS):
+            tiles = slice(c * TILES, (c + 1) * TILES)
+            nc.sync.dma_start(out=hid_sb[:, tiles, :], in_=hid_view[:, tiles, :])
+
+        chunks = []
+        for c in range(REF_CHUNKS):
+            rows = slice(c * CHUNK, (c + 1) * CHUNK)
+            chunks.append((ref_sb[:, c * TILES : (c + 1) * TILES, :], rh_codes[:, :, rows], rh_scales[:, :, rows]))
+        for c in range(HID_CHUNKS):
+            rows = slice(c * CHUNK, (c + 1) * CHUNK)
+            chunks.append((hid_sb[:, c * TILES : (c + 1) * TILES, :], h_codes[:, :, rows], h_scales[:, :, rows]))
+
+        def transposed(c):
+            x_codes = stage.tile([P, PASSES, CHUNK], U32, tag="x_codes", align_bytes=64)
+            x_scales = stage.tile([P, PASSES, CHUNK], U8, tag="x_scales", align_bytes=64)
+            transpose_and_quantise(nc, psum, stage, identity, chunks[c][0], x_codes, x_scales)
+            return x_codes, x_scales
+
+        def scores(c):
+            for j in range(c * TILES, (c + 1) * TILES):
+                for n in range(REF_CHUNKS):
+                    acc = psum.tile([P, CHUNK], F32, tag="bank")
+                    for G in range(PASSES):
+                        nc.tensor.matmul_mx(
+                            out=acc[:],
+                            lhsT=h_codes[:, G, j * P : (j + 1) * P].bitcast(FP8X4),
+                            lhsT_scale=h_scales[:, G, j * P : (j + 1) * P],
+                            rhs=rh_codes[:, G, n * CHUNK : (n + 1) * CHUNK].bitcast(FP8X4),
+                            rhs_scale=rh_scales[:, G, n * CHUNK : (n + 1) * CHUNK],
+                            start=(G == 0),
+                            stop=(G == PASSES - 1),
+                        )
+                    piece = out_sb[:, j, 1 + n * CHUNK : 1 + (n + 1) * CHUNK]
+                    if j % 2 == 0:
+                        nc.vector.tensor_copy(out=piece, in_=acc[:])
+                    else:
+                        nc.scalar.copy(out=piece, in_=acc[:])
+                nc.sync.dma_start(out=out_view[:, j, :], in_=out_sb[:, j, 0:OUT_COLS])
+
+        x_next = transposed(0)
+        nc.vector.tensor_copy(out=bias_rows_f32[:], in_=bias_rows[:])
+        bias_bank = psum.tile([P, CHUNK], F32, tag="bank")
+        nc.tensor.transpose(bias_bank[:, 0:P], bias_rows_f32[:], identity[:])
+        nc.vector.tensor_copy(out=bias[:], in_=bias_bank[:, 0 : D // P])
+
+        for c in range(len(chunks)):
+            x_codes, x_scales = x_next
+            codes, scales = chunks[c][1], chunks[c][2]
+            planes_0 = project(nc, psum, stage, w_codes, w_scales, bias, x_codes, x_scales, 0)
+            if c + 1 < len(chunks):
+                x_next = transposed(c + 1)
+            regroup_and_quantise(nc, stage, planes_0, codes[:, 0, :], scales[:, 0, :])
+            planes_1 = project(nc, psum, stage, w_codes, w_scales, bias, x_codes, x_scales, 1)
+            regroup_and_quantise(nc, stage, planes_1, codes[:, 1, :], scales[:, 1, :])
+            if c > REF_CHUNKS:
+                scores(c - 1 - REF_CHUNKS)
+        scores(HID_CHUNKS - 1)

@@ -20,40 +20,33 @@ N_HID = 1024
 N_REF = 1536
 CHUNK = 512
 TILES = CHUNK // P
-HALF = CHUNK // 2
 REF_CHUNKS = N_REF // CHUNK
 HID_CHUNKS = N_HID // CHUNK
 HID_TILES = N_HID // P
-OUT_COLS = 1 + N_REF
-OUT_PITCH = 1544
+LEAD = 8
 
 FLOPS = 2 * (N_HID + N_REF) * D * D + 2 * N_HID * N_REF * D
 
 
 def transpose_and_quantise(nc, psum, stage, identity, x_rows, x_codes, x_scales):
-    for g in range(PASSES):
-        grouped = stage.tile([P, CHUNK, PACK], BF16, tag="grouped_x", align_bytes=64)
-        for half in range(CHUNK // HALF):
-            bank = psum.tile([P, 2, HALF], F32, tag="bank")
+    for i in range(TILES):
+        words = x_rows[:, i, :].bitcast(F32)
+        bank = psum.tile([P, PASSES, 2, P], F32, tag="bank")
+        for g in range(PASSES):
             for u in range(2):
-                for i in range(HALF // P):
-                    words = x_rows[:, half * (HALF // P) + i, :].bitcast(F32)
-                    nc.tensor.transpose(
-                        bank[:, u, i * P : (i + 1) * P],
-                        words[:, 256 * g + u : 256 * (g + 1) : 2],
-                        identity[:],
-                    )
-            rows = grouped[:, half * HALF : (half + 1) * HALF, :]
-            pairs = rows.rearrange("p r t -> p (r t)").bitcast(F32).rearrange("p (r u) -> p r u", u=2)
-            if half == 0:
-                nc.vector.tensor_copy(out=pairs, in_=bank[:].rearrange("p u r -> p r u"))
-            else:
-                nc.scalar.copy(out=pairs, in_=bank[:].rearrange("p u r -> p r u"))
-        nc.vector.quantize_mx(
-            out=x_codes[:, g, :].bitcast(FP8X4),
-            scales=x_scales[:, g, :],
-            in_=grouped[:].rearrange("p r t -> p (r t)"),
-        )
+                nc.tensor.transpose(bank[:, g, u, :], words[:, 256 * g + u : 256 * (g + 1) : 2], identity[:])
+        grouped = stage.tile([P, PASSES, P * PACK], BF16, tag="grouped_x", align_bytes=64)
+        pairs = grouped[:].bitcast(F32).rearrange("p g (r u) -> p g r u", u=2)
+        if i % 2 == 0:
+            nc.vector.tensor_copy(out=pairs, in_=bank[:].rearrange("p g u r -> p g r u"))
+        else:
+            nc.scalar.copy(out=pairs, in_=bank[:].rearrange("p g u r -> p g r u"))
+        for g in range(PASSES):
+            nc.vector.quantize_mx(
+                out=x_codes[:, g, i * P : (i + 1) * P].bitcast(FP8X4),
+                scales=x_scales[:, g, i * P : (i + 1) * P],
+                in_=grouped[:, g, :],
+            )
 
 
 def project(nc, psum, stage, w_codes, w_scales, bias, x_codes, x_scales, G):
@@ -105,34 +98,33 @@ def tile_trackhead_pa_kernel(tc, hid, ref_hid, W1_words, W1_scales, b1, out):
         rh_scales = keep.tile([P, PASSES, N_REF], U8, align_bytes=64)
         h_codes = keep.tile([P, PASSES, N_HID], U32, align_bytes=64)
         h_scales = keep.tile([P, PASSES, N_HID], U8, align_bytes=64)
-        out_sb = keep.tile([P, HID_TILES, OUT_PITCH], F32)
+        out_sb = keep.tile([P, HID_TILES, LEAD + N_REF], F32)
         identity = keep.tile([P, P], F32)
         bias_rows = keep.tile([P, P], BF16)
         bias_rows_f32 = keep.tile([P, P], F32)
         bias = keep.tile([P, D // P], F32)
 
-        nc.vector.memset(w_scales[:].rearrange("p g n -> p (g n)").bitcast(I32), 0)
         nc.vector.memset(bias_rows[:], 0.0)
+        nc.vector.memset(w_scales[:].rearrange("p g n -> p (g n)").bitcast(I32), 0)
         make_identity(nc, identity[:])
-        nc.gpsimd.memset(out_sb[:, :, 0:8], 0.0)
+        nc.gpsimd.memset(out_sb[:, :, 0:LEAD], 0.0)
 
         ref_view = ref_hid.rearrange("(i p) k -> p i k", p=P)
         hid_view = hid.rearrange("(p j) k -> p j k", j=HID_TILES)
         out_view = out.rearrange("(p j) n -> p j n", j=HID_TILES)
 
+        nc.scalar.dma_start(out=bias_rows[0 : D // P, :], in_=b1.rearrange("(m p) -> m p", p=P))
         for i in range(TILES):
             nc.sync.dma_start(out=ref_sb[:, i, :], in_=ref_view[:, i, :])
-        nc.sync.dma_start(out=bias_rows[0 : D // P, :], in_=b1.rearrange("(m p) -> m p", p=P))
         for Q in range(4):
             nc.sync.dma_start(
                 out=w_scales[32 * Q : 32 * Q + 4, :, :].bitcast(I32),
                 in_=W1_scales[:, 4 * Q : 4 * Q + 4, :].rearrange("g r n -> r g n").bitcast(I32),
             )
-        for g in range(PASSES):
-            nc.sync.dma_start(
-                out=w_codes[:, g, :].bitcast(I32),
-                in_=W1_words[g].rearrange("p n t -> p (n t)").bitcast(I32),
-            )
+        w_view = W1_words.rearrange("g p n t -> p g (n t)").bitcast(I32)
+        for G in range(PASSES):
+            features = slice(G * K_PASS, (G + 1) * K_PASS)
+            nc.sync.dma_start(out=w_codes[:, :, features].bitcast(I32), in_=w_view[:, :, features])
         for i in range(TILES, N_REF // P):
             nc.sync.dma_start(out=ref_sb[:, i, :], in_=ref_view[:, i, :])
         for c in range(HID_CHUNKS):
@@ -167,15 +159,19 @@ def tile_trackhead_pa_kernel(tc, hid, ref_hid, W1_words, W1_scales, b1, out):
                             start=(G == 0),
                             stop=(G == PASSES - 1),
                         )
-                    piece = out_sb[:, j, 1 + n * CHUNK : 1 + (n + 1) * CHUNK]
-                    if j % 2 == 0:
+                    piece = out_sb[:, j, LEAD + n * CHUNK : LEAD + (n + 1) * CHUNK]
+                    if (j * REF_CHUNKS + n) % 2 == 0:
                         nc.vector.tensor_copy(out=piece, in_=acc[:])
                     else:
                         nc.scalar.copy(out=piece, in_=acc[:])
-                nc.sync.dma_start(out=out_view[:, j, :], in_=out_sb[:, j, 0:OUT_COLS])
+                    first = 1 + n * CHUNK if n > 0 else 0
+                    nc.sync.dma_start(
+                        out=out_view[:, j, first : 1 + (n + 1) * CHUNK],
+                        in_=out_sb[:, j, LEAD - 1 + first : LEAD + (n + 1) * CHUNK],
+                    )
 
-        x_next = transposed(0)
         nc.vector.tensor_copy(out=bias_rows_f32[:], in_=bias_rows[:])
+        x_next = transposed(0)
         bias_bank = psum.tile([P, CHUNK], F32, tag="bank")
         nc.tensor.transpose(bias_bank[:, 0:P], bias_rows_f32[:], identity[:])
         nc.vector.tensor_copy(out=bias[:], in_=bias_bank[:, 0 : D // P])

@@ -28,25 +28,20 @@ LEAD = 8
 FLOPS = 2 * (N_HID + N_REF) * D * D + 2 * N_HID * N_REF * D
 
 
-def transpose_and_quantise(nc, psum, stage, identity, x_rows, x_codes, x_scales):
+def transpose_rows(nc, psum, stage, identity, x_rows):
+    grouped = stage.tile([P, PASSES, CHUNK * PACK], BF16, tag="grouped_x", align_bytes=64)
+    pairs = grouped[:].bitcast(F32).rearrange("p g (r u) -> p g r u", u=2)
     for i in range(TILES):
         words = x_rows[:, i, :].bitcast(F32)
         bank = psum.tile([P, PASSES, 2, P], F32, tag="bank")
         for g in range(PASSES):
             for u in range(2):
                 nc.tensor.transpose(bank[:, g, u, :], words[:, 256 * g + u : 256 * (g + 1) : 2], identity[:])
-        grouped = stage.tile([P, PASSES, P * PACK], BF16, tag="grouped_x", align_bytes=64)
-        pairs = grouped[:].bitcast(F32).rearrange("p g (r u) -> p g r u", u=2)
         if i % 2 == 0:
-            nc.vector.tensor_copy(out=pairs, in_=bank[:].rearrange("p g u r -> p g r u"))
+            nc.vector.tensor_copy(out=pairs[:, :, i * P : (i + 1) * P, :], in_=bank[:].rearrange("p g u r -> p g r u"))
         else:
-            nc.scalar.copy(out=pairs, in_=bank[:].rearrange("p g u r -> p g r u"))
-        for g in range(PASSES):
-            nc.vector.quantize_mx(
-                out=x_codes[:, g, i * P : (i + 1) * P].bitcast(FP8X4),
-                scales=x_scales[:, g, i * P : (i + 1) * P],
-                in_=grouped[:, g, :],
-            )
+            nc.scalar.copy(out=pairs[:, :, i * P : (i + 1) * P, :], in_=bank[:].rearrange("p g u r -> p g r u"))
+    return grouped
 
 
 def project(nc, psum, stage, w_codes, w_scales, bias, x_codes, x_scales, G):
@@ -66,20 +61,12 @@ def project(nc, psum, stage, w_codes, w_scales, bias, x_codes, x_scales, G):
                 stop=(g == PASSES - 1),
             )
         nc.scalar.activation(out=planes[:, t, :], in_=acc[:], func=IDENTITY, bias=bias[:, m : m + 1])
-    return planes
-
-
-def regroup_and_quantise(nc, stage, planes, codes, scales):
-    grouped = stage.tile([P, CHUNK, PACK], BF16, tag="grouped_h", align_bytes=64)
+    grouped = stage.tile([P, CHUNK * PACK], BF16, tag="grouped_h", align_bytes=64)
     nc.vector.tensor_copy(
-        out=grouped[:].rearrange("p (c i) t -> p c t i", i=4),
+        out=grouped[:].rearrange("p (c i t) -> p c t i", i=4, t=PACK),
         in_=planes[:].rearrange("p t (c i) -> p c t i", i=4),
     )
-    nc.vector.quantize_mx(
-        out=codes.bitcast(FP8X4),
-        scales=scales,
-        in_=grouped[:].rearrange("p r t -> p (r t)"),
-    )
+    return grouped
 
 
 def tile_trackhead_pa_kernel(tc, hid, ref_hid, W1_words, W1_scales, b1, out):
@@ -104,29 +91,35 @@ def tile_trackhead_pa_kernel(tc, hid, ref_hid, W1_words, W1_scales, b1, out):
         bias_rows_f32 = keep.tile([P, P], F32)
         bias = keep.tile([P, D // P], F32)
 
-        nc.vector.memset(bias_rows[:], 0.0)
         nc.vector.memset(w_scales[:].rearrange("p g n -> p (g n)").bitcast(I32), 0)
         make_identity(nc, identity[:])
+        nc.gpsimd.memset(bias_rows[:], 0.0)
+        nc.gpsimd.dma_start(out=bias_rows[0 : D // P, :], in_=b1.rearrange("(m p) -> m p", p=P))
         nc.gpsimd.memset(out_sb[:, :, 0:LEAD], 0.0)
 
         ref_view = ref_hid.rearrange("(i p) k -> p i k", p=P)
         hid_view = hid.rearrange("(p j) k -> p j k", j=HID_TILES)
         out_view = out.rearrange("(p j) n -> p j n", j=HID_TILES)
+        w_view = W1_words.rearrange("g p n t -> p g (n t)").bitcast(I32)
 
-        nc.scalar.dma_start(out=bias_rows[0 : D // P, :], in_=b1.rearrange("(m p) -> m p", p=P))
-        for i in range(TILES):
-            nc.sync.dma_start(out=ref_sb[:, i, :], in_=ref_view[:, i, :])
+        def load_ref_chunk(c):
+            for i in range(c * TILES, (c + 1) * TILES):
+                nc.sync.dma_start(out=ref_sb[:, i, :], in_=ref_view[:, i, :])
+
+        def load_w_half(G):
+            features = slice(G * K_PASS, (G + 1) * K_PASS)
+            nc.sync.dma_start(out=w_codes[:, :, features].bitcast(I32), in_=w_view[:, :, features])
+
+        load_ref_chunk(0)
         for Q in range(4):
             nc.sync.dma_start(
                 out=w_scales[32 * Q : 32 * Q + 4, :, :].bitcast(I32),
                 in_=W1_scales[:, 4 * Q : 4 * Q + 4, :].rearrange("g r n -> r g n").bitcast(I32),
             )
-        w_view = W1_words.rearrange("g p n t -> p g (n t)").bitcast(I32)
-        for G in range(PASSES):
-            features = slice(G * K_PASS, (G + 1) * K_PASS)
-            nc.sync.dma_start(out=w_codes[:, :, features].bitcast(I32), in_=w_view[:, :, features])
-        for i in range(TILES, N_REF // P):
-            nc.sync.dma_start(out=ref_sb[:, i, :], in_=ref_view[:, i, :])
+        load_w_half(0)
+        load_ref_chunk(1)
+        load_w_half(1)
+        load_ref_chunk(2)
         for c in range(HID_CHUNKS):
             tiles = slice(c * TILES, (c + 1) * TILES)
             nc.sync.dma_start(out=hid_sb[:, tiles, :], in_=hid_view[:, tiles, :])
@@ -138,53 +131,63 @@ def tile_trackhead_pa_kernel(tc, hid, ref_hid, W1_words, W1_scales, b1, out):
         for c in range(HID_CHUNKS):
             rows = slice(c * CHUNK, (c + 1) * CHUNK)
             chunks.append((hid_sb[:, c * TILES : (c + 1) * TILES, :], h_codes[:, :, rows], h_scales[:, :, rows]))
+        n_chunks = len(chunks)
 
-        def transposed(c):
+        def quantise_x(grouped):
             x_codes = stage.tile([P, PASSES, CHUNK], U32, tag="x_codes", align_bytes=64)
             x_scales = stage.tile([P, PASSES, CHUNK], U8, tag="x_scales", align_bytes=64)
-            transpose_and_quantise(nc, psum, stage, identity, chunks[c][0], x_codes, x_scales)
+            for g in range(PASSES):
+                nc.vector.quantize_mx(out=x_codes[:, g, :].bitcast(FP8X4), scales=x_scales[:, g, :], in_=grouped[:, g, :])
             return x_codes, x_scales
 
-        def scores(c):
-            for j in range(c * TILES, (c + 1) * TILES):
-                for n in range(REF_CHUNKS):
-                    acc = psum.tile([P, CHUNK], F32, tag="bank")
-                    for G in range(PASSES):
-                        nc.tensor.matmul_mx(
-                            out=acc[:],
-                            lhsT=h_codes[:, G, j * P : (j + 1) * P].bitcast(FP8X4),
-                            lhsT_scale=h_scales[:, G, j * P : (j + 1) * P],
-                            rhs=rh_codes[:, G, n * CHUNK : (n + 1) * CHUNK].bitcast(FP8X4),
-                            rhs_scale=rh_scales[:, G, n * CHUNK : (n + 1) * CHUNK],
-                            start=(G == 0),
-                            stop=(G == PASSES - 1),
-                        )
-                    piece = out_sb[:, j, LEAD + n * CHUNK : LEAD + (n + 1) * CHUNK]
-                    if (j * REF_CHUNKS + n) % 2 == 0:
-                        nc.vector.tensor_copy(out=piece, in_=acc[:])
-                    else:
-                        nc.scalar.copy(out=piece, in_=acc[:])
-                    first = 1 + n * CHUNK if n > 0 else 0
-                    nc.sync.dma_start(
-                        out=out_view[:, j, first : 1 + (n + 1) * CHUNK],
-                        in_=out_sb[:, j, LEAD - 1 + first : LEAD + (n + 1) * CHUNK],
-                    )
+        def quantise_h(c, halves):
+            for G in range(PASSES):
+                nc.vector.quantize_mx(
+                    out=chunks[c][1][:, G, :].bitcast(FP8X4), scales=chunks[c][2][:, G, :], in_=halves[G][:]
+                )
 
-        nc.vector.tensor_copy(out=bias_rows_f32[:], in_=bias_rows[:])
-        x_next = transposed(0)
+        def store(j, first, end):
+            nc.sync.dma_start(out=out_view[:, j, first:end], in_=out_sb[:, j, LEAD - 1 + first : LEAD - 1 + end])
+
+        x_now = quantise_x(transpose_rows(nc, psum, stage, identity, chunks[0][0]))
+        nc.scalar.copy(out=bias_rows_f32[:], in_=bias_rows[:])
         bias_bank = psum.tile([P, CHUNK], F32, tag="bank")
         nc.tensor.transpose(bias_bank[:, 0:P], bias_rows_f32[:], identity[:])
-        nc.vector.tensor_copy(out=bias[:], in_=bias_bank[:, 0 : D // P])
+        nc.scalar.copy(out=bias[:], in_=bias_bank[:, 0 : D // P])
+        halves = [project(nc, psum, stage, w_codes, w_scales, bias, x_now[0], x_now[1], 0)]
+        for c in range(n_chunks):
+            if c + 1 < n_chunks:
+                x_grouped = transpose_rows(nc, psum, stage, identity, chunks[c + 1][0])
+            if c > 0:
+                quantise_h(c - 1, halves)
+                halves = []
+            if c + 1 < n_chunks:
+                x_next = quantise_x(x_grouped)
+            for G in range(len(halves), PASSES):
+                halves.append(project(nc, psum, stage, w_codes, w_scales, bias, x_now[0], x_now[1], G))
+            x_now = x_next
+        quantise_h(n_chunks - 1, halves)
 
-        for c in range(len(chunks)):
-            x_codes, x_scales = x_next
-            codes, scales = chunks[c][1], chunks[c][2]
-            planes_0 = project(nc, psum, stage, w_codes, w_scales, bias, x_codes, x_scales, 0)
-            if c + 1 < len(chunks):
-                x_next = transposed(c + 1)
-            regroup_and_quantise(nc, stage, planes_0, codes[:, 0, :], scales[:, 0, :])
-            planes_1 = project(nc, psum, stage, w_codes, w_scales, bias, x_codes, x_scales, 1)
-            regroup_and_quantise(nc, stage, planes_1, codes[:, 1, :], scales[:, 1, :])
-            if c > REF_CHUNKS:
-                scores(c - 1 - REF_CHUNKS)
-        scores(HID_CHUNKS - 1)
+        edges = [0] + [1 + (n + 1) * CHUNK for n in range(REF_CHUNKS)]
+        for j in range(HID_TILES):
+            for n in range(REF_CHUNKS):
+                acc = psum.tile([P, CHUNK], F32, tag="bank")
+                for G in range(PASSES):
+                    nc.tensor.matmul_mx(
+                        out=acc[:],
+                        lhsT=h_codes[:, G, j * P : (j + 1) * P].bitcast(FP8X4),
+                        lhsT_scale=h_scales[:, G, j * P : (j + 1) * P],
+                        rhs=rh_codes[:, G, n * CHUNK : (n + 1) * CHUNK].bitcast(FP8X4),
+                        rhs_scale=rh_scales[:, G, n * CHUNK : (n + 1) * CHUNK],
+                        start=(G == 0),
+                        stop=(G == PASSES - 1),
+                    )
+                piece = out_sb[:, j, LEAD + n * CHUNK : LEAD + (n + 1) * CHUNK]
+                if (j * REF_CHUNKS + n) % 2 == 0:
+                    nc.vector.tensor_copy(out=piece, in_=acc[:])
+                else:
+                    nc.scalar.copy(out=piece, in_=acc[:])
+                if j == HID_TILES - 1:
+                    store(j, edges[n], edges[n + 1])
+            if j < HID_TILES - 1:
+                store(j, 0, 1 + N_REF)

@@ -24,6 +24,7 @@ REF_CHUNKS = N_REF // CHUNK
 HID_CHUNKS = N_HID // CHUNK
 HID_TILES = N_HID // P
 LEAD = 8
+FINE_TILES = 2
 
 FLOPS = 2 * (N_HID + N_REF) * D * D + 2 * N_HID * N_REF * D
 
@@ -187,7 +188,7 @@ def tile_trackhead_pa_kernel(tc, hid, ref_hid, W1_words, W1_scales, b1, out):
                     nc.vector.tensor_copy(out=piece, in_=acc[:])
                 else:
                     nc.scalar.copy(out=piece, in_=acc[:])
-                if j == HID_TILES - 1:
+                if j >= HID_TILES - FINE_TILES:
                     store(j, edges[n], edges[n + 1])
-            if j < HID_TILES - 1:
+            if j < HID_TILES - FINE_TILES:
                 store(j, 0, 1 + N_REF)

@@ -24,7 +24,6 @@ REF_CHUNKS = N_REF // CHUNK
 HID_CHUNKS = N_HID // CHUNK
 HID_TILES = N_HID // P
 LEAD = 8
-FINE_TILES = 2
 
 FLOPS = 2 * (N_HID + N_REF) * D * D + 2 * N_HID * N_REF * D
 
@@ -103,24 +102,25 @@ def tile_trackhead_pa_kernel(tc, hid, ref_hid, W1_words, W1_scales, b1, out):
         out_view = out.rearrange("(p j) n -> p j n", j=HID_TILES)
         w_view = W1_words.rearrange("g p n t -> p g (n t)").bitcast(I32)
 
-        def load_ref_chunk(c):
-            for i in range(c * TILES, (c + 1) * TILES):
-                nc.sync.dma_start(out=ref_sb[:, i, :], in_=ref_view[:, i, :])
+        def load_ref_chunk(c, pieces):
+            step = TILES // pieces
+            for i in range(c * TILES, (c + 1) * TILES, step):
+                nc.sync.dma_start(out=ref_sb[:, i : i + step, :], in_=ref_view[:, i : i + step, :])
 
         def load_w_half(G):
             features = slice(G * K_PASS, (G + 1) * K_PASS)
             nc.sync.dma_start(out=w_codes[:, :, features].bitcast(I32), in_=w_view[:, :, features])
 
-        load_ref_chunk(0)
+        load_ref_chunk(0, TILES)
+        load_ref_chunk(1, 2)
         for Q in range(4):
             nc.sync.dma_start(
                 out=w_scales[32 * Q : 32 * Q + 4, :, :].bitcast(I32),
                 in_=W1_scales[:, 4 * Q : 4 * Q + 4, :].rearrange("g r n -> r g n").bitcast(I32),
             )
         load_w_half(0)
-        load_ref_chunk(1)
         load_w_half(1)
-        load_ref_chunk(2)
+        load_ref_chunk(2, 2)
         for c in range(HID_CHUNKS):
             tiles = slice(c * TILES, (c + 1) * TILES)
             nc.sync.dma_start(out=hid_sb[:, tiles, :], in_=hid_view[:, tiles, :])
@@ -150,24 +150,21 @@ def tile_trackhead_pa_kernel(tc, hid, ref_hid, W1_words, W1_scales, b1, out):
         def store(j, first, end):
             nc.sync.dma_start(out=out_view[:, j, first:end], in_=out_sb[:, j, LEAD - 1 + first : LEAD - 1 + end])
 
-        x_now = quantise_x(transpose_rows(nc, psum, stage, identity, chunks[0][0]))
+        x_mx = {}
+        x_mx[0] = quantise_x(transpose_rows(nc, psum, stage, identity, chunks[0][0]))
         nc.scalar.copy(out=bias_rows_f32[:], in_=bias_rows[:])
+        x_mx[1] = quantise_x(transpose_rows(nc, psum, stage, identity, chunks[1][0]))
         bias_bank = psum.tile([P, CHUNK], F32, tag="bank")
         nc.tensor.transpose(bias_bank[:, 0:P], bias_rows_f32[:], identity[:])
         nc.scalar.copy(out=bias[:], in_=bias_bank[:, 0 : D // P])
-        halves = [project(nc, psum, stage, w_codes, w_scales, bias, x_now[0], x_now[1], 0)]
         for c in range(n_chunks):
-            if c + 1 < n_chunks:
-                x_grouped = transpose_rows(nc, psum, stage, identity, chunks[c + 1][0])
-            if c > 0:
-                quantise_h(c - 1, halves)
-                halves = []
-            if c + 1 < n_chunks:
-                x_next = quantise_x(x_grouped)
-            for G in range(len(halves), PASSES):
-                halves.append(project(nc, psum, stage, w_codes, w_scales, bias, x_now[0], x_now[1], G))
-            x_now = x_next
-        quantise_h(n_chunks - 1, halves)
+            x_codes, x_scales = x_mx[c]
+            halves = [project(nc, psum, stage, w_codes, w_scales, bias, x_codes, x_scales, G) for G in range(PASSES)]
+            if c + 2 < n_chunks:
+                x_grouped = transpose_rows(nc, psum, stage, identity, chunks[c + 2][0])
+            quantise_h(c, halves)
+            if c + 2 < n_chunks:
+                x_mx[c + 2] = quantise_x(x_grouped)
 
         edges = [0] + [1 + (n + 1) * CHUNK for n in range(REF_CHUNKS)]
         for j in range(HID_TILES):
@@ -188,7 +185,7 @@ def tile_trackhead_pa_kernel(tc, hid, ref_hid, W1_words, W1_scales, b1, out):
                     nc.vector.tensor_copy(out=piece, in_=acc[:])
                 else:
                     nc.scalar.copy(out=piece, in_=acc[:])
-                if j >= HID_TILES - FINE_TILES:
+                if j == HID_TILES - 1:
                     store(j, edges[n], edges[n + 1])
-            if j < HID_TILES - FINE_TILES:
+            if j < HID_TILES - 1:
                 store(j, 0, 1 + N_REF)

@@ -23,7 +23,8 @@ TILES = CHUNK // P
 REF_CHUNKS = N_REF // CHUNK
 HID_CHUNKS = N_HID // CHUNK
 HID_TILES = N_HID // P
-LEAD = 8
+ROW = 1 + N_REF
+BLOCK = 8
 
 FLOPS = 2 * (N_HID + N_REF) * D * D + 2 * N_HID * N_REF * D
 
@@ -85,7 +86,7 @@ def tile_trackhead_pa_kernel(tc, hid, ref_hid, W1_words, W1_scales, b1, out):
         rh_scales = keep.tile([P, PASSES, N_REF], U8, align_bytes=64)
         h_codes = keep.tile([P, PASSES, N_HID], U32, align_bytes=64)
         h_scales = keep.tile([P, PASSES, N_HID], U8, align_bytes=64)
-        out_sb = keep.tile([P, HID_TILES, LEAD + N_REF], F32)
+        out_sb = keep.tile([P, HID_TILES * ROW], F32)
         identity = keep.tile([P, P], F32)
         bias_rows = keep.tile([P, P], BF16)
         bias_rows_f32 = keep.tile([P, P], F32)
@@ -95,11 +96,11 @@ def tile_trackhead_pa_kernel(tc, hid, ref_hid, W1_words, W1_scales, b1, out):
         make_identity(nc, identity[:])
         nc.gpsimd.memset(bias_rows[:], 0.0)
         nc.gpsimd.dma_start(out=bias_rows[0 : D // P, :], in_=b1.rearrange("(m p) -> m p", p=P))
-        nc.gpsimd.memset(out_sb[:, :, 0:LEAD], 0.0)
+        nc.vector.memset(out_sb[:].rearrange("p (j n) -> p j n", n=ROW)[:, :, 0:1], 0.0)
 
         ref_view = ref_hid.rearrange("(i p) k -> p i k", p=P)
         hid_view = hid.rearrange("(p j) k -> p j k", j=HID_TILES)
-        out_view = out.rearrange("(p j) n -> p j n", j=HID_TILES)
+        out_view = out.rearrange("(p j) n -> p (j n)", j=HID_TILES)
         w_view = W1_words.rearrange("g p n t -> p g (n t)").bitcast(I32)
 
         def load_ref_chunk(c, pieces):
@@ -147,8 +148,8 @@ def tile_trackhead_pa_kernel(tc, hid, ref_hid, W1_words, W1_scales, b1, out):
                     out=chunks[c][1][:, G, :].bitcast(FP8X4), scales=chunks[c][2][:, G, :], in_=halves[G][:]
                 )
 
-        def store(j, first, end):
-            nc.sync.dma_start(out=out_view[:, j, first:end], in_=out_sb[:, j, LEAD - 1 + first : LEAD - 1 + end])
+        def store(first, end):
+            nc.sync.dma_start(out=out_view[:, first:end], in_=out_sb[:, first:end])
 
         x_mx = {}
         x_mx[0] = quantise_x(transpose_rows(nc, psum, stage, identity, chunks[0][0]))
@@ -166,7 +167,7 @@ def tile_trackhead_pa_kernel(tc, hid, ref_hid, W1_words, W1_scales, b1, out):
             if c + 2 < n_chunks:
                 x_mx[c + 2] = quantise_x(x_grouped)
 
-        edges = [0] + [1 + (n + 1) * CHUNK for n in range(REF_CHUNKS)]
+        stored = 0
         for j in range(HID_TILES):
             for n in range(REF_CHUNKS):
                 acc = psum.tile([P, CHUNK], F32, tag="bank")
@@ -180,12 +181,13 @@ def tile_trackhead_pa_kernel(tc, hid, ref_hid, W1_words, W1_scales, b1, out):
                         start=(G == 0),
                         stop=(G == PASSES - 1),
                     )
-                piece = out_sb[:, j, LEAD + n * CHUNK : LEAD + (n + 1) * CHUNK]
+                first = j * ROW + 1 + n * CHUNK
+                piece = out_sb[:, first : first + CHUNK]
                 if (j * REF_CHUNKS + n) % 2 == 0:
                     nc.vector.tensor_copy(out=piece, in_=acc[:])
                 else:
                     nc.scalar.copy(out=piece, in_=acc[:])
-                if j == HID_TILES - 1:
-                    store(j, edges[n], edges[n + 1])
-            if j < HID_TILES - 1:
-                store(j, 0, 1 + N_REF)
+                if j == HID_TILES - 1 or n == REF_CHUNKS - 1:
+                    end = (first + CHUNK) // BLOCK * BLOCK
+                    store(stored, end)
+                    stored = end

@@ -45,27 +45,32 @@ def transpose_rows(nc, psum, stage, identity, x_rows):
     return grouped
 
 
-def project(nc, psum, stage, w_codes, w_scales, bias, x_codes, x_scales, G):
-    planes = stage.tile([P, PACK, CHUNK], BF16, tag="planes")
+def project(nc, psum, stage, w_codes, w_scales, bias, x_codes, x_scales, G, first, width):
+    rows = slice(first, first + width)
+    planes = stage.tile([P, PACK, width], BF16, tag="planes")
     for t in range(PACK):
         m = PACK * G + t
         features = slice(m * P, (m + 1) * P)
-        acc = psum.tile([P, CHUNK], F32, tag="bank")
+        acc = psum.tile([P, width], F32, tag="bank")
         for g in range(PASSES):
             nc.tensor.matmul_mx(
                 out=acc[:],
                 lhsT=w_codes[:, g, features].bitcast(FP8X4),
                 lhsT_scale=w_scales[:, g, features],
-                rhs=x_codes[:, g, :].bitcast(FP8X4),
-                rhs_scale=x_scales[:, g, :],
+                rhs=x_codes[:, g, rows].bitcast(FP8X4),
+                rhs_scale=x_scales[:, g, rows],
                 start=(g == 0),
                 stop=(g == PASSES - 1),
             )
         nc.scalar.activation(out=planes[:, t, :], in_=acc[:], func=IDENTITY, bias=bias[:, m : m + 1])
-    grouped = stage.tile([P, CHUNK * PACK], BF16, tag="grouped_h", align_bytes=64)
+    return planes
+
+
+def group_features(nc, stage, planes, first, width):
+    grouped = stage.tile([P, width * PACK], BF16, tag="grouped_h", align_bytes=64)
     nc.vector.tensor_copy(
         out=grouped[:].rearrange("p (c i t) -> p c t i", i=4, t=PACK),
-        in_=planes[:].rearrange("p t (c i) -> p c t i", i=4),
+        in_=planes[:, :, first : first + width].rearrange("p t (c i) -> p c t i", i=4),
     )
     return grouped
 
@@ -142,33 +147,20 @@ def tile_trackhead_pa_kernel(tc, hid, ref_hid, W1_words, W1_scales, b1, out):
                 nc.vector.quantize_mx(out=x_codes[:, g, :].bitcast(FP8X4), scales=x_scales[:, g, :], in_=grouped[:, g, :])
             return x_codes, x_scales
 
-        def quantise_h(c, halves):
-            for G in range(PASSES):
-                nc.vector.quantize_mx(
-                    out=chunks[c][1][:, G, :].bitcast(FP8X4), scales=chunks[c][2][:, G, :], in_=halves[G][:]
-                )
+        def project_half(c, G, first=0, width=CHUNK):
+            return project(nc, psum, stage, w_codes, w_scales, bias, x_mx[c][0], x_mx[c][1], G, first, width)
+
+        def quantise_h(c, G, grouped, first=0, width=CHUNK):
+            rows = slice(first, first + width)
+            nc.vector.quantize_mx(
+                out=chunks[c][1][:, G, rows].bitcast(FP8X4), scales=chunks[c][2][:, G, rows], in_=grouped[:]
+            )
 
         def store(first, end):
             nc.sync.dma_start(out=out_view[:, first:end], in_=out_sb[:, first:end])
 
-        x_mx = {}
-        x_mx[0] = quantise_x(transpose_rows(nc, psum, stage, identity, chunks[0][0]))
-        nc.scalar.copy(out=bias_rows_f32[:], in_=bias_rows[:])
-        x_mx[1] = quantise_x(transpose_rows(nc, psum, stage, identity, chunks[1][0]))
-        bias_bank = psum.tile([P, CHUNK], F32, tag="bank")
-        nc.tensor.transpose(bias_bank[:, 0:P], bias_rows_f32[:], identity[:])
-        nc.scalar.copy(out=bias[:], in_=bias_bank[:, 0 : D // P])
-        for c in range(n_chunks):
-            x_codes, x_scales = x_mx[c]
-            halves = [project(nc, psum, stage, w_codes, w_scales, bias, x_codes, x_scales, G) for G in range(PASSES)]
-            if c + 2 < n_chunks:
-                x_grouped = transpose_rows(nc, psum, stage, identity, chunks[c + 2][0])
-            quantise_h(c, halves)
-            if c + 2 < n_chunks:
-                x_mx[c + 2] = quantise_x(x_grouped)
-
-        stored = 0
-        for j in range(HID_TILES):
+        def score(j, scalar_alone):
+            stored = j * ROW // BLOCK * BLOCK
             for n in range(REF_CHUNKS):
                 acc = psum.tile([P, CHUNK], F32, tag="bank")
                 for G in range(PASSES):
@@ -183,7 +175,7 @@ def tile_trackhead_pa_kernel(tc, hid, ref_hid, W1_words, W1_scales, b1, out):
                     )
                 first = j * ROW + 1 + n * CHUNK
                 piece = out_sb[:, first : first + CHUNK]
-                if (j * REF_CHUNKS + n) % 2 == 0:
+                if (j * REF_CHUNKS + n) % 2 == 0 and not scalar_alone:
                     nc.vector.tensor_copy(out=piece, in_=acc[:])
                 else:
                     nc.scalar.copy(out=piece, in_=acc[:])
@@ -191,3 +183,34 @@ def tile_trackhead_pa_kernel(tc, hid, ref_hid, W1_words, W1_scales, b1, out):
                     end = (first + CHUNK) // BLOCK * BLOCK
                     store(stored, end)
                     stored = end
+
+        x_mx = {}
+        x_mx[0] = quantise_x(transpose_rows(nc, psum, stage, identity, chunks[0][0]))
+        nc.scalar.copy(out=bias_rows_f32[:], in_=bias_rows[:])
+        x_mx[1] = quantise_x(transpose_rows(nc, psum, stage, identity, chunks[1][0]))
+        bias_bank = psum.tile([P, CHUNK], F32, tag="bank")
+        nc.tensor.transpose(bias_bank[:, 0:P], bias_rows_f32[:], identity[:])
+        nc.scalar.copy(out=bias[:], in_=bias_bank[:, 0 : D // P])
+        for c in range(n_chunks - 2):
+            halves = [group_features(nc, stage, project_half(c, G), 0, CHUNK) for G in range(PASSES)]
+            x_grouped = transpose_rows(nc, psum, stage, identity, chunks[c + 2][0])
+            for G in range(PASSES):
+                quantise_h(c, G, halves[G])
+            x_mx[c + 2] = quantise_x(x_grouped)
+
+        pair = 2 * P
+
+        def group_and_quantise(c, G, planes, first, width):
+            for r in range(0, width, pair):
+                quantise_h(c, G, group_features(nc, stage, planes, r, pair), first + r, pair)
+
+        for G in range(PASSES):
+            group_and_quantise(3, G, project_half(3, G), 0, CHUNK)
+        for G in range(PASSES):
+            group_and_quantise(4, G, project_half(4, G, 0, pair), 0, pair)
+        for j in range(3):
+            score(j, j == 0)
+        for G in range(PASSES):
+            group_and_quantise(4, G, project_half(4, G, pair, pair), pair, pair)
+        for j in range(3, HID_TILES):
+            score(j, j == 3)

@@ -29,16 +29,25 @@ BLOCK = 8
 FLOPS = 2 * (N_HID + N_REF) * D * D + 2 * N_HID * N_REF * D
 
 
-def transpose_rows(nc, psum, stage, identity, x_rows):
+def lay_out_words(nc, stage, x_rows):
+    words = stage.tile([P, TILES, PASSES, 2, P], F32, tag="words")
+    for i in range(0, TILES, 2):
+        nc.vector.tensor_copy(
+            out=words[:, i : i + 2].rearrange("p i g u q -> p (i g) u q"),
+            in_=x_rows[:, i : i + 2, :].bitcast(F32).rearrange("p i (g q u) -> p (i g) u q", g=PASSES, u=2),
+        )
+    return words
+
+
+def transpose_rows(nc, psum, stage, identity, word_of, vector_tiles):
     grouped = stage.tile([P, PASSES, CHUNK * PACK], BF16, tag="grouped_x", align_bytes=64)
     pairs = grouped[:].bitcast(F32).rearrange("p g (r u) -> p g r u", u=2)
     for i in range(TILES):
-        words = x_rows[:, i, :].bitcast(F32)
         bank = psum.tile([P, PASSES, 2, P], F32, tag="bank")
         for g in range(PASSES):
             for u in range(2):
-                nc.tensor.transpose(bank[:, g, u, :], words[:, 256 * g + u : 256 * (g + 1) : 2], identity[:])
-        if i % 2 == 0:
+                nc.tensor.transpose(bank[:, g, u, :], word_of(i, g, u), identity[:])
+        if i in vector_tiles:
             nc.vector.tensor_copy(out=pairs[:, :, i * P : (i + 1) * P, :], in_=bank[:].rearrange("p g u r -> p g r u"))
         else:
             nc.scalar.copy(out=pairs[:, :, i * P : (i + 1) * P, :], in_=bank[:].rearrange("p g u r -> p g r u"))
@@ -140,6 +149,12 @@ def tile_trackhead_pa_kernel(tc, hid, ref_hid, W1_words, W1_scales, b1, out):
             chunks.append((hid_sb[:, c * TILES : (c + 1) * TILES, :], h_codes[:, :, rows], h_scales[:, :, rows]))
         n_chunks = len(chunks)
 
+        def every_second_word(c):
+            return lambda i, g, u: chunks[c][0][:, i, :].bitcast(F32)[:, 256 * g + u : 256 * (g + 1) : 2]
+
+        def transpose_laid_out(words):
+            return transpose_rows(nc, psum, stage, identity, lambda i, g, u: words[:, i, g, u, :], [0])
+
         def quantise_x(grouped):
             x_codes = stage.tile([P, PASSES, CHUNK], U32, tag="x_codes", align_bytes=64)
             x_scales = stage.tile([P, PASSES, CHUNK], U8, tag="x_scales", align_bytes=64)
@@ -185,15 +200,16 @@ def tile_trackhead_pa_kernel(tc, hid, ref_hid, W1_words, W1_scales, b1, out):
                     stored = end
 
         x_mx = {}
-        x_mx[0] = quantise_x(transpose_rows(nc, psum, stage, identity, chunks[0][0]))
+        x_mx[0] = quantise_x(transpose_rows(nc, psum, stage, identity, every_second_word(0), [0, 2]))
         nc.scalar.copy(out=bias_rows_f32[:], in_=bias_rows[:])
-        x_mx[1] = quantise_x(transpose_rows(nc, psum, stage, identity, chunks[1][0]))
+        x_mx[1] = quantise_x(transpose_rows(nc, psum, stage, identity, every_second_word(1), [0, 2]))
         bias_bank = psum.tile([P, CHUNK], F32, tag="bank")
         nc.tensor.transpose(bias_bank[:, 0:P], bias_rows_f32[:], identity[:])
         nc.scalar.copy(out=bias[:], in_=bias_bank[:, 0 : D // P])
         for c in range(n_chunks - 2):
+            words = lay_out_words(nc, stage, chunks[c + 2][0])
             halves = [group_features(nc, stage, project_half(c, G), 0, CHUNK) for G in range(PASSES)]
-            x_grouped = transpose_rows(nc, psum, stage, identity, chunks[c + 2][0])
+            x_grouped = transpose_laid_out(words)
             for G in range(PASSES):
                 quantise_h(c, G, halves[G])
             x_mx[c + 2] = quantise_x(x_grouped)

@@ -21,10 +21,8 @@ N_REF = 1536
 CHUNK = 512
 TILES = CHUNK // P
 REF_CHUNKS = N_REF // CHUNK
-HID_CHUNKS = N_HID // CHUNK
 HID_TILES = N_HID // P
 ROW = 1 + N_REF
-BLOCK = 8
 
 FLOPS = 2 * (N_HID + N_REF) * D * D + 2 * N_HID * N_REF * D
 
@@ -114,20 +112,21 @@ def tile_trackhead_pa_kernel(tc, hid, ref_hid, W1_words, W1_scales, b1, out):
 
         ref_view = ref_hid.rearrange("(i p) k -> p i k", p=P)
         hid_view = hid.rearrange("(p j) k -> p j k", j=HID_TILES)
-        out_view = out.rearrange("(p j) n -> p (j n)", j=HID_TILES)
+        out_view = out.rearrange("(p j) n -> p j n", j=HID_TILES)
+        out_rows = out_sb[:].rearrange("p (j n) -> p j n", n=ROW)
         w_view = W1_words.rearrange("g p n t -> p g (n t)").bitcast(I32)
 
-        def load_ref_chunk(c, pieces):
-            step = TILES // pieces
-            for i in range(c * TILES, (c + 1) * TILES, step):
-                nc.sync.dma_start(out=ref_sb[:, i : i + step, :], in_=ref_view[:, i : i + step, :])
+        def load_rows(tile, view, first, end):
+            nc.sync.dma_start(out=tile[:, first:end, :], in_=view[:, first:end, :])
 
         def load_w_half(G):
             features = slice(G * K_PASS, (G + 1) * K_PASS)
             nc.sync.dma_start(out=w_codes[:, :, features].bitcast(I32), in_=w_view[:, :, features])
 
-        load_ref_chunk(0, TILES)
-        load_ref_chunk(1, 2)
+        for i in range(TILES):
+            load_rows(ref_sb, ref_view, i, i + 1)
+        for i in range(0, TILES, 2):
+            load_rows(hid_sb, hid_view, i, i + 2)
         for Q in range(4):
             nc.sync.dma_start(
                 out=w_scales[32 * Q : 32 * Q + 4, :, :].bitcast(I32),
@@ -135,19 +134,19 @@ def tile_trackhead_pa_kernel(tc, hid, ref_hid, W1_words, W1_scales, b1, out):
             )
         load_w_half(0)
         load_w_half(1)
-        load_ref_chunk(2, 2)
-        for c in range(HID_CHUNKS):
-            tiles = slice(c * TILES, (c + 1) * TILES)
-            nc.sync.dma_start(out=hid_sb[:, tiles, :], in_=hid_view[:, tiles, :])
+        for i in range(TILES, 3 * TILES, 2):
+            load_rows(ref_sb, ref_view, i, i + 2)
+        load_rows(hid_sb, hid_view, TILES, 2 * TILES)
 
-        chunks = []
-        for c in range(REF_CHUNKS):
+        def ref_chunk(c):
             rows = slice(c * CHUNK, (c + 1) * CHUNK)
-            chunks.append((ref_sb[:, c * TILES : (c + 1) * TILES, :], rh_codes[:, :, rows], rh_scales[:, :, rows]))
-        for c in range(HID_CHUNKS):
+            return ref_sb[:, c * TILES : (c + 1) * TILES, :], rh_codes[:, :, rows], rh_scales[:, :, rows]
+
+        def hid_chunk(c):
             rows = slice(c * CHUNK, (c + 1) * CHUNK)
-            chunks.append((hid_sb[:, c * TILES : (c + 1) * TILES, :], h_codes[:, :, rows], h_scales[:, :, rows]))
-        n_chunks = len(chunks)
+            return hid_sb[:, c * TILES : (c + 1) * TILES, :], h_codes[:, :, rows], h_scales[:, :, rows]
+
+        chunks = [ref_chunk(0), hid_chunk(0), ref_chunk(1), ref_chunk(2), hid_chunk(1)]
 
         def every_second_word(c):
             return lambda i, g, u: chunks[c][0][:, i, :].bitcast(F32)[:, 256 * g + u : 256 * (g + 1) : 2]
@@ -171,33 +170,35 @@ def tile_trackhead_pa_kernel(tc, hid, ref_hid, W1_words, W1_scales, b1, out):
                 out=chunks[c][1][:, G, rows].bitcast(FP8X4), scales=chunks[c][2][:, G, rows], in_=grouped[:]
             )
 
-        def store(first, end):
-            nc.sync.dma_start(out=out_view[:, first:end], in_=out_sb[:, first:end])
+        def score(j, n, engine):
+            acc = psum.tile([P, CHUNK], F32, tag="bank")
+            for G in range(PASSES):
+                nc.tensor.matmul_mx(
+                    out=acc[:],
+                    lhsT=h_codes[:, G, j * P : (j + 1) * P].bitcast(FP8X4),
+                    lhsT_scale=h_scales[:, G, j * P : (j + 1) * P],
+                    rhs=rh_codes[:, G, n * CHUNK : (n + 1) * CHUNK].bitcast(FP8X4),
+                    rhs_scale=rh_scales[:, G, n * CHUNK : (n + 1) * CHUNK],
+                    start=(G == 0),
+                    stop=(G == PASSES - 1),
+                )
+            piece = out_rows[:, j, 1 + n * CHUNK : 1 + (n + 1) * CHUNK]
+            if engine is nc.vector:
+                nc.vector.tensor_copy(out=piece, in_=acc[:])
+            else:
+                nc.scalar.copy(out=piece, in_=acc[:])
 
-        def score(j, scalar_alone):
-            stored = j * ROW // BLOCK * BLOCK
-            for n in range(REF_CHUNKS):
-                acc = psum.tile([P, CHUNK], F32, tag="bank")
-                for G in range(PASSES):
-                    nc.tensor.matmul_mx(
-                        out=acc[:],
-                        lhsT=h_codes[:, G, j * P : (j + 1) * P].bitcast(FP8X4),
-                        lhsT_scale=h_scales[:, G, j * P : (j + 1) * P],
-                        rhs=rh_codes[:, G, n * CHUNK : (n + 1) * CHUNK].bitcast(FP8X4),
-                        rhs_scale=rh_scales[:, G, n * CHUNK : (n + 1) * CHUNK],
-                        start=(G == 0),
-                        stop=(G == PASSES - 1),
-                    )
-                first = j * ROW + 1 + n * CHUNK
-                piece = out_sb[:, first : first + CHUNK]
-                if (j * REF_CHUNKS + n) % 2 == 0 and not scalar_alone:
-                    nc.vector.tensor_copy(out=piece, in_=acc[:])
-                else:
-                    nc.scalar.copy(out=piece, in_=acc[:])
-                if j == HID_TILES - 1 or n == REF_CHUNKS - 1:
-                    end = (first + CHUNK) // BLOCK * BLOCK
-                    store(stored, end)
-                    stored = end
+        def store(first_tile, end_tile, first, end):
+            nc.sync.dma_start(
+                out=out_view[:, first_tile:end_tile, first:end], in_=out_rows[:, first_tile:end_tile, first:end]
+            )
+
+        edges = [0] + [1 + (n + 1) * CHUNK for n in range(REF_CHUNKS)]
+
+        def score_first_half(n, engines):
+            for j in range(TILES):
+                score(j, n, engines[j])
+            store(0, TILES, edges[n], edges[n + 1])
 
         x_mx = {}
         x_mx[0] = quantise_x(transpose_rows(nc, psum, stage, identity, every_second_word(0), [0, 2]))
@@ -206,27 +207,37 @@ def tile_trackhead_pa_kernel(tc, hid, ref_hid, W1_words, W1_scales, b1, out):
         bias_bank = psum.tile([P, CHUNK], F32, tag="bank")
         nc.tensor.transpose(bias_bank[:, 0:P], bias_rows_f32[:], identity[:])
         nc.scalar.copy(out=bias[:], in_=bias_bank[:, 0 : D // P])
-        for c in range(n_chunks - 2):
+
+        both = [nc.scalar, nc.scalar, nc.vector, nc.vector]
+
+        for c in range(3):
             words = lay_out_words(nc, stage, chunks[c + 2][0])
             halves = [group_features(nc, stage, project_half(c, G), 0, CHUNK) for G in range(PASSES)]
+            if c == 2:
+                score_first_half(0, both)
             x_grouped = transpose_laid_out(words)
             for G in range(PASSES):
                 quantise_h(c, G, halves[G])
             x_mx[c + 2] = quantise_x(x_grouped)
+        halves = [group_features(nc, stage, project_half(3, G), 0, CHUNK) for G in range(PASSES)]
+        score_first_half(1, both)
+        for G in range(PASSES):
+            quantise_h(3, G, halves[G])
 
         pair = 2 * P
 
-        def group_and_quantise(c, G, planes, first, width):
-            for r in range(0, width, pair):
-                quantise_h(c, G, group_features(nc, stage, planes, r, pair), first + r, pair)
+        def project_pair(first):
+            for G in range(PASSES):
+                quantise_h(4, G, group_features(nc, stage, project_half(4, G, first, pair), 0, pair), first, pair)
 
-        for G in range(PASSES):
-            group_and_quantise(3, G, project_half(3, G), 0, CHUNK)
-        for G in range(PASSES):
-            group_and_quantise(4, G, project_half(4, G, 0, pair), 0, pair)
-        for j in range(3):
-            score(j, j == 0)
-        for G in range(PASSES):
-            group_and_quantise(4, G, project_half(4, G, pair, pair), pair, pair)
-        for j in range(3, HID_TILES):
-            score(j, j == 3)
+        project_pair(0)
+        score_first_half(2, [nc.scalar] * TILES)
+        project_pair(pair)
+        for j in range(TILES, HID_TILES):
+            for n in range(REF_CHUNKS):
+                scalar = j == TILES or (j * REF_CHUNKS + n) % 2 == 1
+                score(j, n, nc.scalar if scalar else nc.vector)
+                if j == HID_TILES - 1:
+                    store(j, j + 1, edges[n], edges[n + 1])
+            if j < HID_TILES - 1:
+                store(j, j + 1, 0, ROW)

@@ -119,21 +119,24 @@ def tile_trackhead_pa_kernel(tc, hid, ref_hid, W1_words, W1_scales, b1, out):
         def load_rows(tile, view, first, end):
             nc.sync.dma_start(out=tile[:, first:end, :], in_=view[:, first:end, :])
 
-        def load_w_half(G):
-            features = slice(G * K_PASS, (G + 1) * K_PASS)
+        def load_w(first, end):
+            features = slice(first, end)
             nc.sync.dma_start(out=w_codes[:, :, features].bitcast(I32), in_=w_view[:, :, features])
 
-        for i in range(TILES):
+        for g in range(PASSES):
+            nc.sync.dma_start(out=ref_sb[:, 0, g * K_PASS : (g + 1) * K_PASS], in_=ref_view[:, 0, g * K_PASS : (g + 1) * K_PASS])
+        for i in range(1, TILES):
             load_rows(ref_sb, ref_view, i, i + 1)
-        for i in range(0, TILES, 2):
-            load_rows(hid_sb, hid_view, i, i + 2)
+        for i in range(TILES):
+            load_rows(hid_sb, hid_view, i, i + 1)
         for Q in range(4):
             nc.sync.dma_start(
                 out=w_scales[32 * Q : 32 * Q + 4, :, :].bitcast(I32),
                 in_=W1_scales[:, 4 * Q : 4 * Q + 4, :].rearrange("g r n -> r g n").bitcast(I32),
             )
-        load_w_half(0)
-        load_w_half(1)
+        load_w(0, 2 * P)
+        load_w(2 * P, K_PASS)
+        load_w(K_PASS, D)
         for i in range(TILES, 3 * TILES, 2):
             load_rows(ref_sb, ref_view, i, i + 2)
         load_rows(hid_sb, hid_view, TILES, 2 * TILES)
@@ -170,35 +173,35 @@ def tile_trackhead_pa_kernel(tc, hid, ref_hid, W1_words, W1_scales, b1, out):
                 out=chunks[c][1][:, G, rows].bitcast(FP8X4), scales=chunks[c][2][:, G, rows], in_=grouped[:]
             )
 
-        def score(j, n, engine):
-            acc = psum.tile([P, CHUNK], F32, tag="bank")
+        def score(j, first, end, engine):
+            acc = psum.tile([P, end - first], F32, tag="bank")
             for G in range(PASSES):
                 nc.tensor.matmul_mx(
                     out=acc[:],
                     lhsT=h_codes[:, G, j * P : (j + 1) * P].bitcast(FP8X4),
                     lhsT_scale=h_scales[:, G, j * P : (j + 1) * P],
-                    rhs=rh_codes[:, G, n * CHUNK : (n + 1) * CHUNK].bitcast(FP8X4),
-                    rhs_scale=rh_scales[:, G, n * CHUNK : (n + 1) * CHUNK],
+                    rhs=rh_codes[:, G, first:end].bitcast(FP8X4),
+                    rhs_scale=rh_scales[:, G, first:end],
                     start=(G == 0),
                     stop=(G == PASSES - 1),
                 )
-            piece = out_rows[:, j, 1 + n * CHUNK : 1 + (n + 1) * CHUNK]
+            piece = out_rows[:, j, 1 + first : 1 + end]
             if engine is nc.vector:
                 nc.vector.tensor_copy(out=piece, in_=acc[:])
             else:
                 nc.scalar.copy(out=piece, in_=acc[:])
 
         def store(first_tile, end_tile, first, end):
+            columns = slice(1 + first if first else 0, 1 + end)
             nc.sync.dma_start(
-                out=out_view[:, first_tile:end_tile, first:end], in_=out_rows[:, first_tile:end_tile, first:end]
+                out=out_view[:, first_tile:end_tile, columns], in_=out_rows[:, first_tile:end_tile, columns]
             )
 
-        edges = [0] + [1 + (n + 1) * CHUNK for n in range(REF_CHUNKS)]
-
         def score_first_half(n, engines):
+            first, end = n * CHUNK, (n + 1) * CHUNK
             for j in range(TILES):
-                score(j, n, engines[j])
-            store(0, TILES, edges[n], edges[n + 1])
+                score(j, first, end, engines[j])
+            store(0, TILES, first, end)
 
         x_mx = {}
         x_mx[0] = quantise_x(transpose_rows(nc, psum, stage, identity, every_second_word(0), [0, 2]))
@@ -226,18 +229,23 @@ def tile_trackhead_pa_kernel(tc, hid, ref_hid, W1_words, W1_scales, b1, out):
 
         pair = 2 * P
 
-        def project_pair(first):
+        def project_pair(first, width):
             for G in range(PASSES):
-                quantise_h(4, G, group_features(nc, stage, project_half(4, G, first, pair), 0, pair), first, pair)
+                planes = project_half(4, G, first, pair)
+                for r in range(0, pair, width):
+                    quantise_h(4, G, group_features(nc, stage, planes, r, width), first + r, width)
 
-        project_pair(0)
-        score_first_half(2, [nc.scalar] * TILES)
-        project_pair(pair)
-        for j in range(TILES, HID_TILES):
+        def score_row(j, engines):
             for n in range(REF_CHUNKS):
-                scalar = j == TILES or (j * REF_CHUNKS + n) % 2 == 1
-                score(j, n, nc.scalar if scalar else nc.vector)
-                if j == HID_TILES - 1:
-                    store(j, j + 1, edges[n], edges[n + 1])
-            if j < HID_TILES - 1:
-                store(j, j + 1, 0, ROW)
+                score(j, n * CHUNK, (n + 1) * CHUNK, engines[n])
+            store(j, j + 1, 0, N_REF)
+
+        project_pair(0, pair)
+        score_first_half(2, [nc.scalar] * TILES)
+        score_row(4, [nc.vector, nc.scalar, nc.vector])
+        project_pair(pair, P)
+        pieces = [(j, n * CHUNK, (n + 1) * CHUNK) for j in (5, 6, 7) for n in range(REF_CHUNKS)]
+        pieces[-1:] = [(7, 2 * CHUNK, 2 * CHUNK + pair), (7, 2 * CHUNK + pair, N_REF)]
+        for i, (j, first, end) in enumerate(pieces):
+            score(j, first, end, nc.scalar if j == 5 or i % 2 == 0 else nc.vector)
+            store(j, j + 1, first, end)

@@ -21,6 +21,7 @@ N_REF = 1536
 CHUNK = 512
 TILES = CHUNK // P
 REF_CHUNKS = N_REF // CHUNK
+HID_CHUNKS = N_HID // CHUNK
 HID_TILES = N_HID // P
 ROW = 1 + N_REF
 
@@ -73,13 +74,11 @@ def project(nc, psum, stage, w_codes, w_scales, bias, x_codes, x_scales, G, firs
     return planes
 
 
-def group_features(nc, stage, planes, first, width):
-    grouped = stage.tile([P, width * PACK], BF16, tag="grouped_h", align_bytes=64)
+def group_features(nc, planes, grouped):
     nc.vector.tensor_copy(
-        out=grouped[:].rearrange("p (c i t) -> p c t i", i=4, t=PACK),
-        in_=planes[:, :, first : first + width].rearrange("p t (c i) -> p c t i", i=4),
+        out=grouped.rearrange("p (c i t) -> p c t i", i=4, t=PACK),
+        in_=planes.rearrange("p t (c i) -> p c t i", i=4),
     )
-    return grouped
 
 
 def tile_trackhead_pa_kernel(tc, hid, ref_hid, W1_words, W1_scales, b1, out):
@@ -94,10 +93,10 @@ def tile_trackhead_pa_kernel(tc, hid, ref_hid, W1_words, W1_scales, b1, out):
         hid_sb = keep.tile([P, HID_TILES, D], BF16)
         w_codes = keep.tile([P, PASSES, D], U32, align_bytes=64)
         w_scales = keep.tile([P, PASSES, D], U8, align_bytes=64)
-        rh_codes = keep.tile([P, PASSES, N_REF], U32, align_bytes=64)
-        rh_scales = keep.tile([P, PASSES, N_REF], U8, align_bytes=64)
-        h_codes = keep.tile([P, PASSES, N_HID], U32, align_bytes=64)
-        h_scales = keep.tile([P, PASSES, N_HID], U8, align_bytes=64)
+        rh_codes = keep.tile([P, REF_CHUNKS, PASSES, CHUNK], U32, align_bytes=64)
+        rh_scales = keep.tile([P, REF_CHUNKS, PASSES, CHUNK], U8, align_bytes=64)
+        h_codes = keep.tile([P, HID_CHUNKS, PASSES, CHUNK], U32, align_bytes=64)
+        h_scales = keep.tile([P, HID_CHUNKS, PASSES, CHUNK], U8, align_bytes=64)
         out_sb = keep.tile([P, HID_TILES * ROW], F32)
         identity = keep.tile([P, P], F32)
         bias_rows = keep.tile([P, P], BF16)
@@ -142,12 +141,10 @@ def tile_trackhead_pa_kernel(tc, hid, ref_hid, W1_words, W1_scales, b1, out):
         load_rows(hid_sb, hid_view, TILES, 2 * TILES)
 
         def ref_chunk(c):
-            rows = slice(c * CHUNK, (c + 1) * CHUNK)
-            return ref_sb[:, c * TILES : (c + 1) * TILES, :], rh_codes[:, :, rows], rh_scales[:, :, rows]
+            return ref_sb[:, c * TILES : (c + 1) * TILES, :], rh_codes[:, c], rh_scales[:, c]
 
         def hid_chunk(c):
-            rows = slice(c * CHUNK, (c + 1) * CHUNK)
-            return hid_sb[:, c * TILES : (c + 1) * TILES, :], h_codes[:, :, rows], h_scales[:, :, rows]
+            return hid_sb[:, c * TILES : (c + 1) * TILES, :], h_codes[:, c], h_scales[:, c]
 
         chunks = [ref_chunk(0), hid_chunk(0), ref_chunk(1), ref_chunk(2), hid_chunk(1)]
 
@@ -157,31 +154,51 @@ def tile_trackhead_pa_kernel(tc, hid, ref_hid, W1_words, W1_scales, b1, out):
         def transpose_laid_out(words):
             return transpose_rows(nc, psum, stage, identity, lambda i, g, u: words[:, i, g, u, :], [0])
 
-        def quantise_x(grouped):
+        def quantise_x(grouped, passes_at_once=PASSES):
             x_codes = stage.tile([P, PASSES, CHUNK], U32, tag="x_codes", align_bytes=64)
             x_scales = stage.tile([P, PASSES, CHUNK], U8, tag="x_scales", align_bytes=64)
-            for g in range(PASSES):
-                nc.vector.quantize_mx(out=x_codes[:, g, :].bitcast(FP8X4), scales=x_scales[:, g, :], in_=grouped[:, g, :])
+            for g in range(0, PASSES, passes_at_once):
+                passes = slice(g, g + passes_at_once)
+                nc.vector.quantize_mx(
+                    out=x_codes[:, passes, :].rearrange("p g r -> p (g r)").bitcast(FP8X4),
+                    scales=x_scales[:, passes, :].rearrange("p g r -> p (g r)"),
+                    in_=grouped[:, passes, :].rearrange("p g r -> p (g r)"),
+                )
             return x_codes, x_scales
 
         def project_half(c, G, first=0, width=CHUNK):
             return project(nc, psum, stage, w_codes, w_scales, bias, x_mx[c][0], x_mx[c][1], G, first, width)
 
-        def quantise_h(c, G, grouped, first=0, width=CHUNK):
-            rows = slice(first, first + width)
+        def project_chunk(c):
+            grouped = stage.tile([P, PASSES, CHUNK * PACK], BF16, tag="grouped_h", align_bytes=64)
+            for G in range(PASSES):
+                planes = project_half(c, G)
+                if G == 1 and c + 3 < len(chunks):
+                    words[c + 3] = lay_out_words(nc, stage, chunks[c + 3][0])
+                if G == 1 and c == 3:
+                    quantise_chunk(c, grouped, slice(0, 1))
+                group_features(nc, planes[:], grouped[:, G, :])
+            return grouped
+
+        def quantise_chunk(c, grouped, passes):
             nc.vector.quantize_mx(
-                out=chunks[c][1][:, G, rows].bitcast(FP8X4), scales=chunks[c][2][:, G, rows], in_=grouped[:]
+                out=chunks[c][1][:, passes, :].rearrange("p g r -> p (g r)").bitcast(FP8X4),
+                scales=chunks[c][2][:, passes, :].rearrange("p g r -> p (g r)"),
+                in_=grouped[:, passes, :].rearrange("p g r -> p (g r)"),
             )
 
         def score(j, first, end, engine):
             acc = psum.tile([P, end - first], F32, tag="bank")
+            cols = slice(j % TILES * P, (j % TILES + 1) * P)
+            n = first // CHUNK
+            rows = slice(first - n * CHUNK, end - n * CHUNK)
             for G in range(PASSES):
                 nc.tensor.matmul_mx(
                     out=acc[:],
-                    lhsT=h_codes[:, G, j * P : (j + 1) * P].bitcast(FP8X4),
-                    lhsT_scale=h_scales[:, G, j * P : (j + 1) * P],
-                    rhs=rh_codes[:, G, first:end].bitcast(FP8X4),
-                    rhs_scale=rh_scales[:, G, first:end],
+                    lhsT=h_codes[:, j // TILES, G, cols].bitcast(FP8X4),
+                    lhsT_scale=h_scales[:, j // TILES, G, cols],
+                    rhs=rh_codes[:, n, G, rows].bitcast(FP8X4),
+                    rhs_scale=rh_scales[:, n, G, rows],
                     start=(G == 0),
                     stop=(G == PASSES - 1),
                 )
@@ -204,7 +221,7 @@ def tile_trackhead_pa_kernel(tc, hid, ref_hid, W1_words, W1_scales, b1, out):
             store(0, TILES, first, end)
 
         x_mx = {}
-        x_mx[0] = quantise_x(transpose_rows(nc, psum, stage, identity, every_second_word(0), [0, 2]))
+        x_mx[0] = quantise_x(transpose_rows(nc, psum, stage, identity, every_second_word(0), [0, 2]), 1)
         nc.scalar.copy(out=bias_rows_f32[:], in_=bias_rows[:])
         x_mx[1] = quantise_x(transpose_rows(nc, psum, stage, identity, every_second_word(1), [0, 2]))
         bias_bank = psum.tile([P, CHUNK], F32, tag="bank")
@@ -213,27 +230,33 @@ def tile_trackhead_pa_kernel(tc, hid, ref_hid, W1_words, W1_scales, b1, out):
 
         both = [nc.scalar, nc.scalar, nc.vector, nc.vector]
 
+        words = {2: lay_out_words(nc, stage, chunks[2][0])}
         for c in range(3):
-            words = lay_out_words(nc, stage, chunks[c + 2][0])
-            halves = [group_features(nc, stage, project_half(c, G), 0, CHUNK) for G in range(PASSES)]
+            h_grouped = project_chunk(c)
             if c == 2:
                 score_first_half(0, both)
-            x_grouped = transpose_laid_out(words)
-            for G in range(PASSES):
-                quantise_h(c, G, halves[G])
+            x_grouped = transpose_laid_out(words[c + 2])
+            quantise_chunk(c, h_grouped, slice(0, PASSES))
             x_mx[c + 2] = quantise_x(x_grouped)
-        halves = [group_features(nc, stage, project_half(3, G), 0, CHUNK) for G in range(PASSES)]
+        h_grouped = project_chunk(3)
         score_first_half(1, both)
-        for G in range(PASSES):
-            quantise_h(3, G, halves[G])
+        quantise_chunk(3, h_grouped, slice(1, PASSES))
 
         pair = 2 * P
 
         def project_pair(first, width):
             for G in range(PASSES):
                 planes = project_half(4, G, first, pair)
+                grouped = stage.tile([P, pair * PACK], BF16, tag="grouped_pair", align_bytes=64)
                 for r in range(0, pair, width):
-                    quantise_h(4, G, group_features(nc, stage, planes, r, width), first + r, width)
+                    group_features(nc, planes[:, :, r : r + width], grouped[:, r * PACK : (r + width) * PACK])
+                for r in range(0, pair, width):
+                    rows = slice(first + r, first + r + width)
+                    nc.vector.quantize_mx(
+                        out=chunks[4][1][:, G, rows].bitcast(FP8X4),
+                        scales=chunks[4][2][:, G, rows],
+                        in_=grouped[:, r * PACK : (r + width) * PACK],
+                    )
 
         def score_row(j, engines):
             for n in range(REF_CHUNKS):

@@ -173,11 +173,11 @@ def tile_trackhead_pa_kernel(tc, hid, ref_hid, W1_words, W1_scales, b1, out):
             grouped = stage.tile([P, PASSES, CHUNK * PACK], BF16, tag="grouped_h", align_bytes=64)
             for G in range(PASSES):
                 planes = project_half(c, G)
-                if G == 1 and c + 3 < len(chunks):
-                    words[c + 3] = lay_out_words(nc, stage, chunks[c + 3][0])
                 if G == 1 and c == 3:
                     quantise_chunk(c, grouped, slice(0, 1))
                 group_features(nc, planes[:], grouped[:, G, :])
+            if c + 3 < len(chunks):
+                words[c + 3] = lay_out_words(nc, stage, chunks[c + 3][0])
             return grouped
 
         def quantise_chunk(c, grouped, passes):
@@ -264,8 +264,8 @@ def tile_trackhead_pa_kernel(tc, hid, ref_hid, W1_words, W1_scales, b1, out):
             store(j, j + 1, 0, N_REF)
 
         project_pair(0, pair)
-        score_first_half(2, [nc.scalar] * TILES)
-        score_row(4, [nc.vector, nc.scalar, nc.vector])
+        score_first_half(2, both)
+        score_row(4, [nc.vector] * REF_CHUNKS)
         project_pair(pair, P)
         pieces = [(j, n * CHUNK, (n + 1) * CHUNK) for j in (5, 6, 7) for n in range(REF_CHUNKS)]
         pieces[-1:] = [(7, 2 * CHUNK, 2 * CHUNK + pair), (7, 2 * CHUNK + pair, N_REF)]

from contextlib import ExitStack

import concourse.mybir as mybir
from concourse.masks import make_identity

F32 = mybir.dt.float32
BF16 = mybir.dt.bfloat16
I32 = mybir.dt.int32
U32 = mybir.dt.uint32
U8 = mybir.dt.uint8
FP8X4 = mybir.dt.float8_e4m3fn_x4
IDENTITY = mybir.ActivationFunctionType.Identity

P = 128
PACK = 4
K_PASS = P * PACK
D = 1024
PASSES = D // K_PASS
N_HID = 1024
N_REF = 1536
CHUNK = 512
TILES = CHUNK // P
REF_CHUNKS = N_REF // CHUNK
HID_CHUNKS = N_HID // CHUNK
HID_TILES = N_HID // P
ROW = 1 + N_REF

FLOPS = 2 * (N_HID + N_REF) * D * D + 2 * N_HID * N_REF * D


def lay_out_words(nc, stage, x_rows):
    words = stage.tile([P, TILES, PASSES, 2, P], F32, tag="words")
    for i in range(0, TILES, 2):
        nc.vector.tensor_copy(
            out=words[:, i : i + 2].rearrange("p i g u q -> p (i g) u q"),
            in_=x_rows[:, i : i + 2, :].bitcast(F32).rearrange("p i (g q u) -> p (i g) u q", g=PASSES, u=2),
        )
    return words


def transpose_rows(nc, psum, stage, identity, word_of, vector_tiles):
    grouped = stage.tile([P, PASSES, CHUNK * PACK], BF16, tag="grouped_x", align_bytes=64)
    pairs = grouped[:].bitcast(F32).rearrange("p g (r u) -> p g r u", u=2)
    for i in range(TILES):
        bank = psum.tile([P, PASSES, 2, P], F32, tag="bank")
        for g in range(PASSES):
            for u in range(2):
                nc.tensor.transpose(bank[:, g, u, :], word_of(i, g, u), identity[:])
        if i in vector_tiles:
            nc.vector.tensor_copy(out=pairs[:, :, i * P : (i + 1) * P, :], in_=bank[:].rearrange("p g u r -> p g r u"))
        else:
            nc.scalar.copy(out=pairs[:, :, i * P : (i + 1) * P, :], in_=bank[:].rearrange("p g u r -> p g r u"))
    return grouped


def project(nc, psum, stage, w_codes, w_scales, bias, x_codes, x_scales, G, first, width):
    rows = slice(first, first + width)
    planes = stage.tile([P, PACK, width], BF16, tag="planes")
    for t in range(PACK):
        m = PACK * G + t
        features = slice(m * P, (m + 1) * P)
        acc = psum.tile([P, width], F32, tag="bank")
        for g in range(PASSES):
            nc.tensor.matmul_mx(
                out=acc[:],
                lhsT=w_codes[:, g, features].bitcast(FP8X4),
                lhsT_scale=w_scales[:, g, features],
                rhs=x_codes[:, g, rows].bitcast(FP8X4),
                rhs_scale=x_scales[:, g, rows],
                start=(g == 0),
                stop=(g == PASSES - 1),
            )
        nc.scalar.activation(out=planes[:, t, :], in_=acc[:], func=IDENTITY, bias=bias[:, m : m + 1])
    return planes


def group_features(nc, planes, grouped):
    nc.vector.tensor_copy(
        out=grouped.rearrange("p (c i t) -> p c t i", i=4, t=PACK),
        in_=planes.rearrange("p t (c i) -> p c t i", i=4),
    )


def tile_trackhead_pa_kernel(tc, hid, ref_hid, W1_words, W1_scales, b1, out):
    nc = tc.nc
    with ExitStack() as ctx:
        keep = ctx.enter_context(tc.tile_pool(name="keep", bufs=1))
        stage = ctx.enter_context(tc.tile_pool(name="stage", bufs=3))
        psum = ctx.enter_context(tc.psum_pool(name="psum", bufs=8))
        ctx.enter_context(tc.manual_schedule())

        ref_sb = keep.tile([P, N_REF // P, D], BF16)
        hid_sb = keep.tile([P, HID_TILES, D], BF16)
        w_codes = keep.tile([P, PASSES, D], U32, align_bytes=64)
        w_scales = keep.tile([P, PASSES, D], U8, align_bytes=64)
        rh_codes = keep.tile([P, REF_CHUNKS, PASSES, CHUNK], U32, align_bytes=64)
        rh_scales = keep.tile([P, REF_CHUNKS, PASSES, CHUNK], U8, align_bytes=64)
        h_codes = keep.tile([P, HID_CHUNKS, PASSES, CHUNK], U32, align_bytes=64)
        h_scales = keep.tile([P, HID_CHUNKS, PASSES, CHUNK], U8, align_bytes=64)
        out_sb = keep.tile([P, HID_TILES * ROW], F32)
        identity = keep.tile([P, P], F32)
        bias_rows = keep.tile([P, P], BF16)
        bias_rows_f32 = keep.tile([P, P], F32)
        bias = keep.tile([P, D // P], F32)

        nc.vector.memset(w_scales[:].rearrange("p g n -> p (g n)").bitcast(I32), 0)
        make_identity(nc, identity[:])
        nc.gpsimd.memset(bias_rows[:], 0.0)
        nc.gpsimd.dma_start(out=bias_rows[0 : D // P, :], in_=b1.rearrange("(m p) -> m p", p=P))
        nc.vector.memset(out_sb[:].rearrange("p (j n) -> p j n", n=ROW)[:, :, 0:1], 0.0)

        ref_view = ref_hid.rearrange("(i p) k -> p i k", p=P)
        hid_view = hid.rearrange("(p j) k -> p j k", j=HID_TILES)
        out_view = out.rearrange("(p j) n -> p j n", j=HID_TILES)
        out_rows = out_sb[:].rearrange("p (j n) -> p j n", n=ROW)
        w_view = W1_words.rearrange("g p n t -> p g (n t)").bitcast(I32)

        def load_rows(tile, view, first, end):
            nc.sync.dma_start(out=tile[:, first:end, :], in_=view[:, first:end, :])

        def load_w(first, end):
            features = slice(first, end)
            nc.sync.dma_start(out=w_codes[:, :, features].bitcast(I32), in_=w_view[:, :, features])

        for g in range(PASSES):
            nc.sync.dma_start(out=ref_sb[:, 0, g * K_PASS : (g + 1) * K_PASS], in_=ref_view[:, 0, g * K_PASS : (g + 1) * K_PASS])
        for i in range(1, TILES):
            load_rows(ref_sb, ref_view, i, i + 1)
        for i in range(TILES):
            load_rows(hid_sb, hid_view, i, i + 1)
        for Q in range(4):
            nc.sync.dma_start(
                out=w_scales[32 * Q : 32 * Q + 4, :, :].bitcast(I32),
                in_=W1_scales[:, 4 * Q : 4 * Q + 4, :].rearrange("g r n -> r g n").bitcast(I32),
            )
        load_w(0, 2 * P)
        load_w(2 * P, K_PASS)
        load_w(K_PASS, D)
        for i in range(TILES, 3 * TILES, 2):
            load_rows(ref_sb, ref_view, i, i + 2)
        load_rows(hid_sb, hid_view, TILES, 2 * TILES)

        def ref_chunk(c):
            return ref_sb[:, c * TILES : (c + 1) * TILES, :], rh_codes[:, c], rh_scales[:, c]

        def hid_chunk(c):
            return hid_sb[:, c * TILES : (c + 1) * TILES, :], h_codes[:, c], h_scales[:, c]

        chunks = [ref_chunk(0), hid_chunk(0), ref_chunk(1), ref_chunk(2), hid_chunk(1)]

        def every_second_word(c):
            return lambda i, g, u: chunks[c][0][:, i, :].bitcast(F32)[:, 256 * g + u : 256 * (g + 1) : 2]

        def transpose_laid_out(words):
            return transpose_rows(nc, psum, stage, identity, lambda i, g, u: words[:, i, g, u, :], [0])

        def quantise_x(grouped, passes_at_once=PASSES):
            x_codes = stage.tile([P, PASSES, CHUNK], U32, tag="x_codes", align_bytes=64)
            x_scales = stage.tile([P, PASSES, CHUNK], U8, tag="x_scales", align_bytes=64)
            for g in range(0, PASSES, passes_at_once):
                passes = slice(g, g + passes_at_once)
                nc.vector.quantize_mx(
                    out=x_codes[:, passes, :].rearrange("p g r -> p (g r)").bitcast(FP8X4),
                    scales=x_scales[:, passes, :].rearrange("p g r -> p (g r)"),
                    in_=grouped[:, passes, :].rearrange("p g r -> p (g r)"),
                )
            return x_codes, x_scales

        def project_half(c, G, first=0, width=CHUNK):
            return project(nc, psum, stage, w_codes, w_scales, bias, x_mx[c][0], x_mx[c][1], G, first, width)

        def project_chunk(c):
            grouped = stage.tile([P, PASSES, CHUNK * PACK], BF16, tag="grouped_h", align_bytes=64)
            for G in range(PASSES):
                planes = project_half(c, G)
                if G == 1 and c == 3:
                    quantise_chunk(c, grouped, slice(0, 1))
                group_features(nc, planes[:], grouped[:, G, :])
            if c + 3 < len(chunks):
                words[c + 3] = lay_out_words(nc, stage, chunks[c + 3][0])
            return grouped

        def quantise_chunk(c, grouped, passes):
            nc.vector.quantize_mx(
                out=chunks[c][1][:, passes, :].rearrange("p g r -> p (g r)").bitcast(FP8X4),
                scales=chunks[c][2][:, passes, :].rearrange("p g r -> p (g r)"),
                in_=grouped[:, passes, :].rearrange("p g r -> p (g r)"),
            )

        def score(j, first, end, engine):
            acc = psum.tile([P, end - first], F32, tag="bank")
            cols = slice(j % TILES * P, (j % TILES + 1) * P)
            n = first // CHUNK
            rows = slice(first - n * CHUNK, end - n * CHUNK)
            for G in range(PASSES):
                nc.tensor.matmul_mx(
                    out=acc[:],
                    lhsT=h_codes[:, j // TILES, G, cols].bitcast(FP8X4),
                    lhsT_scale=h_scales[:, j // TILES, G, cols],
                    rhs=rh_codes[:, n, G, rows].bitcast(FP8X4),
                    rhs_scale=rh_scales[:, n, G, rows],
                    start=(G == 0),
                    stop=(G == PASSES - 1),
                )
            piece = out_rows[:, j, 1 + first : 1 + end]
            if engine is nc.vector:
                nc.vector.tensor_copy(out=piece, in_=acc[:])
            else:
                nc.scalar.copy(out=piece, in_=acc[:])

        def store(first_tile, end_tile, first, end):
            columns = slice(1 + first if first else 0, 1 + end)
            nc.sync.dma_start(
                out=out_view[:, first_tile:end_tile, columns], in_=out_rows[:, first_tile:end_tile, columns]
            )

        def score_first_half(n, engines):
            first, end = n * CHUNK, (n + 1) * CHUNK
            for j in range(TILES):
                score(j, first, end, engines[j])
            store(0, TILES, first, end)

        x_mx = {}
        x_mx[0] = quantise_x(transpose_rows(nc, psum, stage, identity, every_second_word(0), [0, 2]), 1)
        nc.scalar.copy(out=bias_rows_f32[:], in_=bias_rows[:])
        x_mx[1] = quantise_x(transpose_rows(nc, psum, stage, identity, every_second_word(1), [0, 2]))
        bias_bank = psum.tile([P, CHUNK], F32, tag="bank")
        nc.tensor.transpose(bias_bank[:, 0:P], bias_rows_f32[:], identity[:])
        nc.scalar.copy(out=bias[:], in_=bias_bank[:, 0 : D // P])

        both = [nc.scalar, nc.scalar, nc.vector, nc.vector]

        words = {2: lay_out_words(nc, stage, chunks[2][0])}
        for c in range(3):
            h_grouped = project_chunk(c)
            if c == 2:
                score_first_half(0, both)
            x_grouped = transpose_laid_out(words[c + 2])
            quantise_chunk(c, h_grouped, slice(0, PASSES))
            x_mx[c + 2] = quantise_x(x_grouped)
        h_grouped = project_chunk(3)
        score_first_half(1, both)
        quantise_chunk(3, h_grouped, slice(1, PASSES))

        pair = 2 * P

        def project_pair(first, width):
            for G in range(PASSES):
                planes = project_half(4, G, first, pair)
                grouped = stage.tile([P, pair * PACK], BF16, tag="grouped_pair", align_bytes=64)
                for r in range(0, pair, width):
                    group_features(nc, planes[:, :, r : r + width], grouped[:, r * PACK : (r + width) * PACK])
                for r in range(0, pair, width):
                    rows = slice(first + r, first + r + width)
                    nc.vector.quantize_mx(
                        out=chunks[4][1][:, G, rows].bitcast(FP8X4),
                        scales=chunks[4][2][:, G, rows],
                        in_=grouped[:, r * PACK : (r + width) * PACK],
                    )

        def score_row(j, engines):
            for n in range(REF_CHUNKS):
                score(j, n * CHUNK, (n + 1) * CHUNK, engines[n])
            store(j, j + 1, 0, N_REF)

        project_pair(0, pair)
        score_first_half(2, both)
        score_row(4, [nc.vector] * REF_CHUNKS)
        project_pair(pair, P)
        pieces = [(j, n * CHUNK, (n + 1) * CHUNK) for j in (5, 6, 7) for n in range(REF_CHUNKS)]
        pieces[-1:] = [(7, 2 * CHUNK, 2 * CHUNK + pair), (7, 2 * CHUNK + pair, N_REF)]
        for i, (j, first, end) in enumerate(pieces):
            score(j, first, end, nc.scalar if j == 5 or i % 2 == 0 else nc.vector)
            store(j, j + 1, first, end)
